import numpy as np
import ml_dtypes


def mxq(x, axis, fmt="e4m3"):
    dtype, down = {"e4m3": (ml_dtypes.float8_e4m3fn, 7), "e5m2": (ml_dtypes.float8_e5m2, 14)}[fmt]
    v = np.moveaxis(np.asarray(x, np.float32).astype(ml_dtypes.bfloat16).astype(np.float64), axis, -1)
    blocks = v.reshape(v.shape[:-1] + (-1, 32))
    amax = np.abs(blocks).max(-1, keepdims=True)
    byte = np.maximum(np.where(amax > 0, np.frexp(amax)[1] - 1 + 127, 0) - down, 1)
    scale = np.exp2(byte - 127.0)
    codes = (blocks / scale).astype(np.float32).astype(dtype).astype(np.float64)
    return np.moveaxis((codes * scale).reshape(v.shape), -1, axis)


WIDE = False


def mx_kscale(k):
    if not WIDE:
        return np.ones(k)
    levels = np.array([10, -10, 5, -5, 0])
    a = np.random.permutation(np.resize(levels, k // 512 * 4)).reshape(k // 512, 4)
    idx = np.arange(k)
    return np.exp2(a[idx // 512, idx % 128 // 32])


BF16 = ml_dtypes.bfloat16


def bf(x):
    return np.asarray(x, np.float32).astype(BF16)


def f64(x):
    return np.asarray(x).astype(np.float64)


B, J, I, O = 512, 2, 512, 128
IN_CH = J * I
OUT_CH = J * O
NEIGHBOUR_LIST = [[j for j in (i - 1, i, i + 1) if 0 <= j < J] for i in range(J)]


def build_mask():
    mask = np.zeros((OUT_CH, IN_CH))
    for i, neigh in enumerate(NEIGHBOUR_LIST):
        mask[i * O:(i + 1) * O, neigh[0] * I:(neigh[-1] + 1) * I] = 1.0
    return mask


def setup_inputs():
    s = mx_kscale(IN_CH)
    keep = np.random.random((OUT_CH, IN_CH)) < 0.75
    return {"x": bf(np.random.standard_normal((B, IN_CH)) * s),
            "weight": bf(np.random.standard_normal((OUT_CH, IN_CH)) / np.sqrt(0.75 * 3 * I) / s[None, :]),
            "mask": bf(build_mask() * keep),
            "bias": bf(np.random.standard_normal(OUT_CH) * 0.5)}


def reference(x, weight, mask, bias):
    x2 = f64(x).reshape(x.shape[0], -1)
    w = f64(weight) * f64(mask)
    xq = mxq(x2, 1, "e4m3")
    cols = []
    for i, neigh in enumerate(NEIGHBOUR_LIST):
        lo, hi = neigh[0] * I, (neigh[-1] + 1) * I
        cols.append(xq[:, lo:hi] @ mxq(w[i * O:(i + 1) * O, lo:hi], 1, "e4m3").T)
    return np.concatenate(cols, axis=1) + f64(bias)

@@ -1,0 +1,129 @@
+from contextlib import ExitStack
+
+import concourse.mybir as mybir
+from concourse.masks import make_identity
+
+F32 = mybir.dt.float32
+BF16 = mybir.dt.bfloat16
+U32 = mybir.dt.uint32
+U8 = mybir.dt.uint8
+FP8X4 = mybir.dt.float8_e4m3fn_x4
+
+P = 128
+PACK = 4
+K_PASS = P * PACK
+HALVES = 2
+
+B, K, O = 512, 1024, 256
+PASSES = K // K_PASS
+B_TILES = B // P
+O_TILES = O // P
+
+FLOPS = 2 * B * K * O
+
+
+def transpose_rows(nc, banks, rows, identity):
+    words = rows.bitcast(F32)
+    bank = banks.tile([P, PASSES, HALVES, P], F32)
+    for g in range(PASSES):
+        for u in range(HALVES):
+            first = (g * HALVES + u) * P
+            nc.tensor.transpose(bank[:, g, u, :], words[:, first : first + P], identity)
+    return bank
+
+
+def word_view(grouped):
+    return grouped.bitcast(F32).rearrange("p (g c u) -> p g c u", g=PASSES, u=HALVES)
+
+
+def tile_skeletonlinear_s_kernel(tc, x, weight, mask, bias, out):
+    nc = tc.nc
+    x_tiles = x.rearrange("(p t) k -> t p k", t=B_TILES)
+    out_tiles = out.rearrange("(p t) o -> t p o", t=B_TILES)
+    weight_tiles = weight.rearrange("(t p) k -> t p k", p=P)
+    mask_tiles = mask.rearrange("(t p) k -> t p k", p=P)
+
+    with ExitStack() as ctx:
+        keep = ctx.enter_context(tc.tile_pool(name="keep", bufs=1))
+        w_pool = ctx.enter_context(tc.tile_pool(name="w_pool", bufs=O_TILES))
+        x_pool = ctx.enter_context(tc.tile_pool(name="x_pool", bufs=B_TILES))
+        banks = ctx.enter_context(tc.psum_pool(name="banks", bufs=4))
+        sums = ctx.enter_context(tc.psum_pool(name="sums", bufs=4))
+
+        weight_rows = []
+        mask_rows = []
+        for j in range(O_TILES):
+            weight_j = w_pool.tile([P, K], BF16)
+            nc.sync.dma_start(out=weight_j[:], in_=weight_tiles[j])
+            weight_rows.append(weight_j)
+            mask_j = w_pool.tile([P, K], BF16)
+            nc.sync.dma_start(out=mask_j[:], in_=mask_tiles[j])
+            mask_rows.append(mask_j)
+        x_rows = []
+        for t in range(B_TILES):
+            x_t = x_pool.tile([P, K], BF16)
+            nc.sync.dma_start(out=x_t[:], in_=x_tiles[t])
+            x_rows.append(x_t)
+
+        identity = keep.tile([P, P], F32)
+        make_identity(nc, identity[:])
+
+        ones = keep.tile([P, P], BF16)
+        nc.vector.memset(ones[:], 1.0)
+        bias_rows = keep.tile([P, O], BF16)
+        nc.vector.memset(bias_rows[:], 0.0)
+        nc.scalar.dma_start(out=bias_rows[0:1, :], in_=bias.unsqueeze(0))
+        bias_sum = sums.tile([P, O], F32, tag="sum")
+        nc.tensor.matmul(out=bias_sum[:], lhsT=ones[:], rhs=bias_rows[:], start=True, stop=True)
+        bias_all = keep.tile([P, O], F32)
+        nc.scalar.copy(out=bias_all[:], in_=bias_sum[:])
+
+        w_grouped = keep.tile([P, PASSES * O * PACK], BF16, align_bytes=64)
+        for j in range(O_TILES):
+            w_j = w_pool.tile([P, K], BF16)
+            nc.vector.tensor_mul(out=w_j[:], in0=weight_rows[j][:], in1=mask_rows[j][:])
+            bank = transpose_rows(nc, banks, w_j[:], identity[:])
+            nc.scalar.copy(
+                out=word_view(w_grouped[:])[:, :, j * P : (j + 1) * P, :],
+                in_=bank[:].rearrange("p g u c -> p g c u"),
+            )
+        w_codes = keep.tile([P, PASSES, O], U32, align_bytes=64)
+        w_scales = keep.tile([P, PASSES, O], U8, align_bytes=64)
+        nc.vector.quantize_mx(
+            out=w_codes[:].rearrange("p g c -> p (g c)").bitcast(FP8X4),
+            scales=w_scales[:].rearrange("p g c -> p (g c)"),
+            in_=w_grouped[:],
+        )
+
+        x_codes = []
+        x_scales = []
+        for t in range(B_TILES):
+            bank = transpose_rows(nc, banks, x_rows[t][:], identity[:])
+            x_grouped = x_pool.tile([P, PASSES * P * PACK], BF16, align_bytes=64)
+            copy_out = nc.vector.tensor_copy if t % 2 == 0 else nc.scalar.copy
+            copy_out(out=word_view(x_grouped[:]), in_=bank[:].rearrange("p g u c -> p g c u"))
+            codes_t = x_pool.tile([P, PASSES, P], U32, align_bytes=64)
+            scales_t = x_pool.tile([P, PASSES, P], U8, align_bytes=64)
+            nc.vector.quantize_mx(
+                out=codes_t[:].rearrange("p g c -> p (g c)").bitcast(FP8X4),
+                scales=scales_t[:].rearrange("p g c -> p (g c)"),
+                in_=x_grouped[:],
+            )
+            x_codes.append(codes_t)
+            x_scales.append(scales_t)
+
+        for t in range(B_TILES):
+            acc = sums.tile([P, O], F32, tag="sum")
+            for g in range(PASSES):
+                nc.tensor.matmul_mx(
+                    out=acc[:],
+                    lhsT=x_codes[t][:, g, :].bitcast(FP8X4),
+                    lhsT_scale=x_scales[t][:, g, :],
+                    rhs=w_codes[:, g, :].bitcast(FP8X4),
+                    rhs_scale=w_scales[:, g, :],
+                    start=(g == 0),
+                    stop=(g == PASSES - 1),
+                )
+            result = x_pool.tile([P, O], F32)
+            nc.vector.tensor_add(out=result[:], in0=acc[:], in1=bias_all[:])
+            nc.sync.dma_start(out=out_tiles[t], in_=result[:])

@@ -50,6 +50,11 @@ def tile_skeletonlinear_s_kernel(tc, x, weight, mask, bias, out):
         banks = ctx.enter_context(tc.psum_pool(name="banks", bufs=4))
         sums = ctx.enter_context(tc.psum_pool(name="sums", bufs=4))
 
+        bias_rows = keep.tile([P, O], BF16)
+        nc.vector.memset(bias_rows[:], 0.0)
+        ones = keep.tile([P, P], BF16)
+        nc.vector.memset(ones[:], 1.0)
+
         weight_rows = []
         mask_rows = []
         for j in range(O_TILES):
@@ -59,6 +64,8 @@ def tile_skeletonlinear_s_kernel(tc, x, weight, mask, bias, out):
             mask_j = w_pool.tile([P, K], BF16)
             nc.sync.dma_start(out=mask_j[:], in_=mask_tiles[j])
             mask_rows.append(mask_j)
+            if j == 0:
+                nc.sync.dma_start(out=bias_rows[0:1, :], in_=bias.unsqueeze(0))
         x_rows = []
         for t in range(B_TILES):
             x_t = x_pool.tile([P, K], BF16)
@@ -67,16 +74,6 @@ def tile_skeletonlinear_s_kernel(tc, x, weight, mask, bias, out):
 
         identity = keep.tile([P, P], F32)
         make_identity(nc, identity[:])
-
-        ones = keep.tile([P, P], BF16)
-        nc.vector.memset(ones[:], 1.0)
-        bias_rows = keep.tile([P, O], BF16)
-        nc.vector.memset(bias_rows[:], 0.0)
-        nc.scalar.dma_start(out=bias_rows[0:1, :], in_=bias.unsqueeze(0))
-        bias_sum = sums.tile([P, O], F32, tag="sum")
-        nc.tensor.matmul(out=bias_sum[:], lhsT=ones[:], rhs=bias_rows[:], start=True, stop=True)
-        bias_all = keep.tile([P, O], F32)
-        nc.scalar.copy(out=bias_all[:], in_=bias_sum[:])
 
         w_grouped = keep.tile([P, PASSES * O * PACK], BF16, align_bytes=64)
         for j in range(O_TILES):
@@ -87,6 +84,11 @@ def tile_skeletonlinear_s_kernel(tc, x, weight, mask, bias, out):
                 out=word_view(w_grouped[:])[:, :, j * P : (j + 1) * P, :],
                 in_=bank[:].rearrange("p g u c -> p g c u"),
             )
+            if j == 0:
+                bias_sum = sums.tile([P, O], F32, tag="sum")
+                nc.tensor.matmul(out=bias_sum[:], lhsT=ones[:], rhs=bias_rows[:], start=True, stop=True)
+                bias_all = keep.tile([P, O], F32)
+                nc.scalar.copy(out=bias_all[:], in_=bias_sum[:])
         w_codes = keep.tile([P, PASSES, O], U32, align_bytes=64)
         w_scales = keep.tile([P, PASSES, O], U8, align_bytes=64)
         nc.vector.quantize_mx(

@@ -22,105 +22,109 @@ O_TILES = O // P
 FLOPS = 2 * B * K * O
 
 
-def transpose_rows(nc, banks, rows, identity):
+def load_rows(nc, loads, source):
+    rows = loads.tile([P, K], BF16)
+    nc.sync.dma_start(out=rows[:], in_=source)
+    return rows
+
+
+def transpose_and_regroup(nc, banks, rows, identity, grouped):
     words = rows.bitcast(F32)
     bank = banks.tile([P, PASSES, HALVES, P], F32)
     for g in range(PASSES):
         for u in range(HALVES):
             first = (g * HALVES + u) * P
             nc.tensor.transpose(bank[:, g, u, :], words[:, first : first + P], identity)
-    return bank
+    nc.scalar.copy(out=grouped, in_=bank[:].rearrange("p g u c -> p g c u"))
 
 
 def word_view(grouped):
     return grouped.bitcast(F32).rearrange("p (g c u) -> p g c u", g=PASSES, u=HALVES)
 
 
+def quantise(nc, pool, grouped, rows):
+    codes = pool.tile([P, PASSES, rows], U32, align_bytes=64)
+    scales = pool.tile([P, PASSES, rows], U8, align_bytes=64)
+    nc.vector.quantize_mx(
+        out=codes[:].rearrange("p g c -> p (g c)").bitcast(FP8X4),
+        scales=scales[:].rearrange("p g c -> p (g c)"),
+        in_=grouped,
+    )
+    return codes, scales
+
+
 def tile_skeletonlinear_s_kernel(tc, x, weight, mask, bias, out):
     nc = tc.nc
     x_tiles = x.rearrange("(p t) k -> t p k", t=B_TILES)
     out_tiles = out.rearrange("(p t) o -> t p o", t=B_TILES)
-    weight_tiles = weight.rearrange("(t p) k -> t p k", p=P)
-    mask_tiles = mask.rearrange("(t p) k -> t p k", p=P)
+    weight_tiles = weight.rearrange("(j p) k -> j p k", p=P)
+    mask_tiles = mask.rearrange("(j p) k -> j p k", p=P)
 
     with ExitStack() as ctx:
         keep = ctx.enter_context(tc.tile_pool(name="keep", bufs=1))
+        loads = ctx.enter_context(tc.tile_pool(name="loads", bufs=B_TILES + 2 * O_TILES))
         w_pool = ctx.enter_context(tc.tile_pool(name="w_pool", bufs=O_TILES))
         x_pool = ctx.enter_context(tc.tile_pool(name="x_pool", bufs=B_TILES))
         banks = ctx.enter_context(tc.psum_pool(name="banks", bufs=4))
         sums = ctx.enter_context(tc.psum_pool(name="sums", bufs=4))
+        ctx.enter_context(tc.manual_schedule())
 
         bias_rows = keep.tile([P, O], BF16)
         nc.vector.memset(bias_rows[:], 0.0)
         ones = keep.tile([P, P], BF16)
         nc.vector.memset(ones[:], 1.0)
-
-        weight_rows = []
-        mask_rows = []
-        for j in range(O_TILES):
-            weight_j = w_pool.tile([P, K], BF16)
-            nc.sync.dma_start(out=weight_j[:], in_=weight_tiles[j])
-            weight_rows.append(weight_j)
-            mask_j = w_pool.tile([P, K], BF16)
-            nc.sync.dma_start(out=mask_j[:], in_=mask_tiles[j])
-            mask_rows.append(mask_j)
-            if j == 0:
-                nc.sync.dma_start(out=bias_rows[0:1, :], in_=bias.unsqueeze(0))
-        x_rows = []
-        for t in range(B_TILES):
-            x_t = x_pool.tile([P, K], BF16)
-            nc.sync.dma_start(out=x_t[:], in_=x_tiles[t])
-            x_rows.append(x_t)
-
         identity = keep.tile([P, P], F32)
         make_identity(nc, identity[:])
 
-        w_grouped = keep.tile([P, PASSES * O * PACK], BF16, align_bytes=64)
+        x_rows = [load_rows(nc, loads, x_tiles[0])]
+        nc.sync.dma_start(out=bias_rows[0:1, :], in_=bias.unsqueeze(0))
+        weight_rows = []
+        mask_rows = []
         for j in range(O_TILES):
+            weight_rows.append(load_rows(nc, loads, weight_tiles[j]))
+            mask_rows.append(load_rows(nc, loads, mask_tiles[j]))
+        for t in range(1, B_TILES):
+            x_rows.append(load_rows(nc, loads, x_tiles[t]))
+
+        x_grouped = []
+        for t in range(B_TILES):
+            grouped_t = x_pool.tile([P, PASSES * P * PACK], BF16, align_bytes=64)
+            x_grouped.append(grouped_t)
+        w_grouped = keep.tile([P, PASSES * O * PACK], BF16, align_bytes=64)
+
+        def masked_weight_tile(j):
             w_j = w_pool.tile([P, K], BF16)
-            nc.vector.tensor_mul(out=w_j[:], in0=weight_rows[j][:], in1=mask_rows[j][:])
-            bank = transpose_rows(nc, banks, w_j[:], identity[:])
-            nc.scalar.copy(
-                out=word_view(w_grouped[:])[:, :, j * P : (j + 1) * P, :],
-                in_=bank[:].rearrange("p g u c -> p g c u"),
+            for g in range(PASSES):
+                k_pass = slice(g * K_PASS, (g + 1) * K_PASS)
+                nc.vector.tensor_mul(
+                    out=w_j[:, k_pass], in0=weight_rows[j][:, k_pass], in1=mask_rows[j][:, k_pass]
+                )
+            transpose_and_regroup(
+                nc, banks, w_j[:], identity[:], word_view(w_grouped[:])[:, :, j * P : (j + 1) * P, :]
             )
-            if j == 0:
-                bias_sum = sums.tile([P, O], F32, tag="sum")
-                nc.tensor.matmul(out=bias_sum[:], lhsT=ones[:], rhs=bias_rows[:], start=True, stop=True)
-                bias_all = keep.tile([P, O], F32)
-                nc.scalar.copy(out=bias_all[:], in_=bias_sum[:])
-        w_codes = keep.tile([P, PASSES, O], U32, align_bytes=64)
-        w_scales = keep.tile([P, PASSES, O], U8, align_bytes=64)
-        nc.vector.quantize_mx(
-            out=w_codes[:].rearrange("p g c -> p (g c)").bitcast(FP8X4),
-            scales=w_scales[:].rearrange("p g c -> p (g c)"),
-            in_=w_grouped[:],
-        )
 
-        x_codes = []
-        x_scales = []
-        for t in range(B_TILES):
-            bank = transpose_rows(nc, banks, x_rows[t][:], identity[:])
-            x_grouped = x_pool.tile([P, PASSES * P * PACK], BF16, align_bytes=64)
-            copy_out = nc.vector.tensor_copy if t % 2 == 0 else nc.scalar.copy
-            copy_out(out=word_view(x_grouped[:]), in_=bank[:].rearrange("p g u c -> p g c u"))
-            codes_t = x_pool.tile([P, PASSES, P], U32, align_bytes=64)
-            scales_t = x_pool.tile([P, PASSES, P], U8, align_bytes=64)
-            nc.vector.quantize_mx(
-                out=codes_t[:].rearrange("p g c -> p (g c)").bitcast(FP8X4),
-                scales=scales_t[:].rearrange("p g c -> p (g c)"),
-                in_=x_grouped[:],
-            )
-            x_codes.append(codes_t)
-            x_scales.append(scales_t)
+        transpose_and_regroup(nc, banks, x_rows[0][:], identity[:], word_view(x_grouped[0][:]))
+        masked_weight_tile(0)
+        bias_sum = sums.tile([P, O], F32, tag="sum")
+        nc.tensor.matmul(out=bias_sum[:], lhsT=ones[:], rhs=bias_rows[:], start=True, stop=True)
+        bias_all = keep.tile([P, O], F32)
+        nc.scalar.copy(out=bias_all[:], in_=bias_sum[:])
+        masked_weight_tile(1)
+
+        x_mx = [quantise(nc, x_pool, x_grouped[0][:], P)]
+        w_codes, w_scales = quantise(nc, keep, w_grouped[:], O)
+        for t in range(1, B_TILES):
+            transpose_and_regroup(nc, banks, x_rows[t][:], identity[:], word_view(x_grouped[t][:]))
+            x_mx.append(quantise(nc, x_pool, x_grouped[t][:], P))
 
         for t in range(B_TILES):
+            x_codes, x_scales = x_mx[t]
             acc = sums.tile([P, O], F32, tag="sum")
             for g in range(PASSES):
                 nc.tensor.matmul_mx(
                     out=acc[:],
-                    lhsT=x_codes[t][:, g, :].bitcast(FP8X4),
-                    lhsT_scale=x_scales[t][:, g, :],
+                    lhsT=x_codes[:, g, :].bitcast(FP8X4),
+                    lhsT_scale=x_scales[:, g, :],
                     rhs=w_codes[:, g, :].bitcast(FP8X4),
                     rhs_scale=w_scales[:, g, :],
                     start=(g == 0),

from contextlib import ExitStack

import concourse.mybir as mybir
from concourse.masks import make_identity

F32 = mybir.dt.float32
BF16 = mybir.dt.bfloat16
U32 = mybir.dt.uint32
U8 = mybir.dt.uint8
FP8X4 = mybir.dt.float8_e4m3fn_x4

P = 128
PACK = 4
K_PASS = P * PACK
HALVES = 2

B, K, O = 512, 1024, 256
PASSES = K // K_PASS
B_TILES = B // P
O_TILES = O // P

FLOPS = 2 * B * K * O


def load_rows(nc, loads, source):
    rows = loads.tile([P, K], BF16)
    nc.sync.dma_start(out=rows[:], in_=source)
    return rows


def transpose_and_regroup(nc, banks, rows, identity, grouped):
    words = rows.bitcast(F32)
    bank = banks.tile([P, PASSES, HALVES, P], F32)
    for g in range(PASSES):
        for u in range(HALVES):
            first = (g * HALVES + u) * P
            nc.tensor.transpose(bank[:, g, u, :], words[:, first : first + P], identity)
    nc.scalar.copy(out=grouped, in_=bank[:].rearrange("p g u c -> p g c u"))


def word_view(grouped):
    return grouped.bitcast(F32).rearrange("p (g c u) -> p g c u", g=PASSES, u=HALVES)


def quantise(nc, pool, grouped, rows):
    codes = pool.tile([P, PASSES, rows], U32, align_bytes=64)
    scales = pool.tile([P, PASSES, rows], U8, align_bytes=64)
    nc.vector.quantize_mx(
        out=codes[:].rearrange("p g c -> p (g c)").bitcast(FP8X4),
        scales=scales[:].rearrange("p g c -> p (g c)"),
        in_=grouped,
    )
    return codes, scales


def tile_skeletonlinear_s_kernel(tc, x, weight, mask, bias, out):
    nc = tc.nc
    x_tiles = x.rearrange("(p t) k -> t p k", t=B_TILES)
    out_tiles = out.rearrange("(p t) o -> t p o", t=B_TILES)
    weight_tiles = weight.rearrange("(j p) k -> j p k", p=P)
    mask_tiles = mask.rearrange("(j p) k -> j p k", p=P)

    with ExitStack() as ctx:
        keep = ctx.enter_context(tc.tile_pool(name="keep", bufs=1))
        loads = ctx.enter_context(tc.tile_pool(name="loads", bufs=B_TILES + 2 * O_TILES))
        w_pool = ctx.enter_context(tc.tile_pool(name="w_pool", bufs=O_TILES))
        x_pool = ctx.enter_context(tc.tile_pool(name="x_pool", bufs=B_TILES))
        banks = ctx.enter_context(tc.psum_pool(name="banks", bufs=4))
        sums = ctx.enter_context(tc.psum_pool(name="sums", bufs=4))
        ctx.enter_context(tc.manual_schedule())

        bias_rows = keep.tile([P, O], BF16)
        nc.vector.memset(bias_rows[:], 0.0)
        ones = keep.tile([P, P], BF16)
        nc.vector.memset(ones[:], 1.0)
        identity = keep.tile([P, P], F32)
        make_identity(nc, identity[:])

        x_rows = [load_rows(nc, loads, x_tiles[0])]
        nc.sync.dma_start(out=bias_rows[0:1, :], in_=bias.unsqueeze(0))
        weight_rows = []
        mask_rows = []
        for j in range(O_TILES):
            weight_rows.append(load_rows(nc, loads, weight_tiles[j]))
            mask_rows.append(load_rows(nc, loads, mask_tiles[j]))
        for t in range(1, B_TILES):
            x_rows.append(load_rows(nc, loads, x_tiles[t]))

        x_grouped = []
        for t in range(B_TILES):
            grouped_t = x_pool.tile([P, PASSES * P * PACK], BF16, align_bytes=64)
            x_grouped.append(grouped_t)
        w_grouped = keep.tile([P, PASSES * O * PACK], BF16, align_bytes=64)

        def masked_weight_tile(j):
            w_j = w_pool.tile([P, K], BF16)
            for g in range(PASSES):
                k_pass = slice(g * K_PASS, (g + 1) * K_PASS)
                nc.vector.tensor_mul(
                    out=w_j[:, k_pass], in0=weight_rows[j][:, k_pass], in1=mask_rows[j][:, k_pass]
                )
            transpose_and_regroup(
                nc, banks, w_j[:], identity[:], word_view(w_grouped[:])[:, :, j * P : (j + 1) * P, :]
            )

        transpose_and_regroup(nc, banks, x_rows[0][:], identity[:], word_view(x_grouped[0][:]))
        masked_weight_tile(0)
        bias_sum = sums.tile([P, O], F32, tag="sum")
        nc.tensor.matmul(out=bias_sum[:], lhsT=ones[:], rhs=bias_rows[:], start=True, stop=True)
        bias_all = keep.tile([P, O], F32)
        nc.scalar.copy(out=bias_all[:], in_=bias_sum[:])
        masked_weight_tile(1)

        x_mx = [quantise(nc, x_pool, x_grouped[0][:], P)]
        w_codes, w_scales = quantise(nc, keep, w_grouped[:], O)
        for t in range(1, B_TILES):
            transpose_and_regroup(nc, banks, x_rows[t][:], identity[:], word_view(x_grouped[t][:]))
            x_mx.append(quantise(nc, x_pool, x_grouped[t][:], P))

        for t in range(B_TILES):
            x_codes, x_scales = x_mx[t]
            acc = sums.tile([P, O], F32, tag="sum")
            for g in range(PASSES):
                nc.tensor.matmul_mx(
                    out=acc[:],
                    lhsT=x_codes[:, g, :].bitcast(FP8X4),
                    lhsT_scale=x_scales[:, g, :],
                    rhs=w_codes[:, g, :].bitcast(FP8X4),
                    rhs_scale=w_scales[:, g, :],
                    start=(g == 0),
                    stop=(g == PASSES - 1),
                )
            result = x_pool.tile([P, O], F32)
            nc.vector.tensor_add(out=result[:], in0=acc[:], in1=bias_all[:])
            nc.sync.dma_start(out=out_tiles[t], in_=result[:])
